import numpy as np
import ml_dtypes


def mxq(x, axis, fmt="e4m3"):
    dtype, down = {"e4m3": (ml_dtypes.float8_e4m3fn, 7), "e5m2": (ml_dtypes.float8_e5m2, 14)}[fmt]
    v = np.moveaxis(np.asarray(x, np.float32).astype(ml_dtypes.bfloat16).astype(np.float64), axis, -1)
    blocks = v.reshape(v.shape[:-1] + (-1, 32))
    amax = np.abs(blocks).max(-1, keepdims=True)
    byte = np.maximum(np.where(amax > 0, np.frexp(amax)[1] - 1 + 127, 0) - down, 1)
    scale = np.exp2(byte - 127.0)
    codes = (blocks / scale).astype(np.float32).astype(dtype).astype(np.float64)
    return np.moveaxis((codes * scale).reshape(v.shape), -1, axis)


WIDE = False


def mx_kscale(k):
    if not WIDE:
        return np.ones(k)
    levels = np.array([20, -20, 10, -10, 0])
    a = np.random.permutation(np.resize(levels, k // 512 * 4)).reshape(k // 512, 4)
    idx = np.arange(k)
    return np.exp2(a[idx // 512, idx % 128 // 32])


BF16 = ml_dtypes.bfloat16


def bf(x):
    return np.asarray(x, np.float32).astype(BF16)


def f64(x):
    return np.asarray(x).astype(np.float64)


B, Nb1, Nw1, Nb2x, Nb2y, Nw2x, Nw2y, R, C = 512, 2, 16, 1, 1, 16, 16, 128, 2
J1 = Nb1 * Nb1
J3 = Nb2x * Nb2y
J2 = J3 * J1
K3 = J1 * R
L3 = C * Nw2x * Nw2y


def to_grid(y):
    y = y.reshape(B, Nb2x, Nb2y, Nw2x, Nw2y, C).transpose(0, 1, 3, 2, 4, 5)
    return y.reshape(B, Nb2x * Nw2x, Nb2y * Nw2y, C)


def from_grid(g):
    g = g.reshape(B, Nb2x, Nw2x, Nb2y, Nw2y, C).transpose(0, 1, 3, 2, 4, 5)
    return g.reshape(B, J3, L3)


def setup_inputs():
    u = mx_kscale(L3)
    h_switch = np.random.standard_normal((B, J2, R))
    k2 = np.random.standard_normal((J2, R, R)) / np.sqrt(R)
    b2 = np.random.standard_normal((1, J2, R)) * 0.3
    k3 = np.random.standard_normal((J3, K3, L3)) / np.sqrt(K3) / u[None, None, :]
    b3 = np.random.standard_normal((1, J3, L3)) * 0.3
    g = np.random.standard_normal((B, J3, L3)) * np.exp2(np.random.randint(-12, 1, (B, 1, 1))) * 4.0 * u[None, None, :]
    return {"h_switch": bf(h_switch), "k2": bf(k2), "b2": bf(b2), "k3": bf(k3), "b3": bf(b3),
            "grad_out": bf(to_grid(g))}


def reference(h_switch, k2, b2, k3, b3, grad_out):
    dy = from_grid(f64(grad_out))
    dyq = mxq(dy, 2, "e5m2").transpose(1, 0, 2)
    k3q = mxq(f64(k3), 2, "e4m3").transpose(0, 2, 1)
    dg = (dyq @ k3q).transpose(1, 0, 2)
    dg = dg.reshape(B, J2, R)
    dh = dg.transpose(1, 0, 2) @ f64(k2).transpose(0, 2, 1)
    return dh.transpose(1, 0, 2)

@@ -1,0 +1,152 @@
+from contextlib import ExitStack
+
+import concourse.mybir as mybir
+from concourse.masks import make_identity
+
+F32 = mybir.dt.float32
+BF16 = mybir.dt.bfloat16
+U32 = mybir.dt.uint32
+U8 = mybir.dt.uint8
+E4M3_X4 = mybir.dt.float8_e4m3fn_x4
+E5M2_X4 = mybir.dt.float8_e5m2_x4
+
+P = 128
+SAMPLES = 512
+WINDOW = 512
+GROUPS = 4
+COEFFS = 128
+ROW_TILES = SAMPLES // P
+WORDS = WINDOW // 2
+HALVES = WORDS // P
+PACK = 4
+
+FLOPS = 2 * SAMPLES * WINDOW * GROUPS * COEFFS + 2 * SAMPLES * GROUPS * COEFFS * COEFFS
+BYTES = 2 * (SAMPLES * WINDOW + GROUPS * COEFFS * WINDOW + GROUPS * COEFFS * COEFFS) + 4 * SAMPLES * GROUPS * COEFFS
+
+
+def transpose_row_tile(nc, bank, words, identity):
+    for u in range(HALVES):
+        nc.tensor.transpose(out=bank[:, u, :], in_=words[:, u * P : (u + 1) * P], identity=identity)
+
+
+def tile_switchnet_fstar_pb_s_kernel(tc, h_switch, k2, b2, k3, b3, grad_out, out):
+    nc = tc.nc
+    with ExitStack() as ctx:
+        keep = ctx.enter_context(tc.tile_pool(name="keep", bufs=1))
+        banks = ctx.enter_context(tc.psum_pool(name="banks", bufs=8))
+
+        dy_rows = grad_out.rearrange("(p t) x y c -> p t (x y c)", t=ROW_TILES)
+        k3_rows = k3.rearrange("o (j p) l -> p (o j) l", p=P)
+        k2_rows = k2.rearrange("j (q t) r -> (j q) (t r)", t=GROUPS)
+        out_rows = out.rearrange("(p t) j r -> p t (j r)", t=ROW_TILES)
+
+        dy_sb = keep.tile([P, ROW_TILES * WINDOW], BF16)
+        k3_sb = keep.tile([P, GROUPS * WINDOW], BF16)
+        k2_sb = keep.tile([P, GROUPS * COEFFS], BF16)
+        dy_sb_tiles = dy_sb[:].rearrange("p (t l) -> p t l", t=ROW_TILES)
+        for h in range(2):
+            nc.sync.dma_start(out=dy_sb_tiles[:, 2 * h : 2 * h + 2, :], in_=dy_rows[:, 2 * h : 2 * h + 2, :])
+        nc.sync.dma_start(out=k3_sb[:, 0:WINDOW], in_=k3_rows[:, 0, :])
+        nc.sync.dma_start(out=k2_sb[:], in_=k2_rows)
+        for j in range(1, GROUPS):
+            nc.sync.dma_start(out=k3_sb[:, j * WINDOW : (j + 1) * WINDOW], in_=k3_rows[:, j, :])
+
+        identity_f32 = keep.tile([P, P], F32)
+        make_identity(nc, identity_f32[:])
+        identity_bf16 = keep.tile([P, P], BF16)
+        nc.vector.tensor_copy(out=identity_bf16[:], in_=identity_f32[:])
+
+        dy_words = dy_sb[:].bitcast(F32)
+        dy_grouped = keep.tile([P, SAMPLES * PACK], BF16, align_bytes=64)
+        dy_grouped_words = dy_grouped[:].bitcast(F32)
+        dy_codes = keep.tile([P, SAMPLES], U32, align_bytes=64)
+        dy_scales = keep.tile([P, SAMPLES], U8, align_bytes=64)
+        for h in range(2):
+            dy_bank = banks.tile([P, 2, HALVES, P], F32, tag="bank")
+            for t in range(2):
+                first_word = (2 * h + t) * WORDS
+                transpose_row_tile(nc, dy_bank[:, t], dy_words[:, first_word : first_word + WORDS], identity_f32[:])
+            nc.scalar.copy(
+                out=dy_grouped_words[:, 2 * h * WORDS : (2 * h + 2) * WORDS].rearrange(
+                    "p (t r u) -> p t r u", t=2, u=HALVES
+                ),
+                in_=dy_bank[:].rearrange("p t u r -> p t r u"),
+            )
+            cols = slice(2 * h * P, (2 * h + 2) * P)
+            nc.vector.quantize_mx(
+                out=dy_codes[:, cols].bitcast(E5M2_X4),
+                scales=dy_scales[:, cols],
+                in_=dy_grouped[:, 2 * h * P * PACK : (2 * h + 2) * P * PACK],
+            )
+
+        k3_words = k3_sb[:].bitcast(F32)
+        k3_grouped = keep.tile([P, GROUPS * COEFFS * PACK], BF16, align_bytes=64)
+        k3_grouped_words = k3_grouped[:].bitcast(F32)
+        k3_codes = keep.tile([P, GROUPS * COEFFS], U32, align_bytes=64)
+        k3_scales = keep.tile([P, GROUPS * COEFFS], U8, align_bytes=64)
+        k2T = keep.tile([P, GROUPS * COEFFS], F32)
+        for j in range(GROUPS):
+            k3_bank = banks.tile([P, HALVES, P], F32, tag="bank")
+            transpose_row_tile(nc, k3_bank, k3_words[:, j * WORDS : (j + 1) * WORDS], identity_f32[:])
+            nc.scalar.copy(
+                out=k3_grouped_words[:, j * WORDS : (j + 1) * WORDS].rearrange("p (r u) -> p r u", u=HALVES),
+                in_=k3_bank[:].rearrange("p u r -> p r u"),
+            )
+            cols = slice(j * COEFFS, (j + 1) * COEFFS)
+            nc.vector.quantize_mx(
+                out=k3_codes[:, cols].bitcast(E4M3_X4),
+                scales=k3_scales[:, cols],
+                in_=k3_grouped[:, j * COEFFS * PACK : (j + 1) * COEFFS * PACK],
+            )
+            if j == 0:
+                k2_bank = banks.tile([P, GROUPS, P], BF16, tag="bank")
+                for t in range(GROUPS):
+                    nc.tensor.transpose(
+                        out=k2_bank[:, t, :], in_=k2_sb[:, t * COEFFS : (t + 1) * COEFFS], identity=identity_bf16[:]
+                    )
+                nc.scalar.copy(
+                    out=k2T[:].rearrange("r (p t) -> r p t", t=GROUPS), in_=k2_bank[:].rearrange("r t p -> r p t")
+                )
+
+        dgT = []
+        for j in range(GROUPS):
+            cols = slice(j * COEFFS, (j + 1) * COEFFS)
+            dg_bank = banks.tile([P, SAMPLES], F32, tag="bank")
+            nc.tensor.matmul_mx(
+                out=dg_bank[:],
+                lhsT=k3_codes[:, cols].bitcast(E4M3_X4),
+                lhsT_scale=k3_scales[:, cols],
+                rhs=dy_codes[:].bitcast(E5M2_X4),
+                rhs_scale=dy_scales[:],
+                start=True,
+                stop=True,
+            )
+            dgT_j = keep.tile([P, SAMPLES], F32, name="dgT%d" % j)
+            if j % 2 == 0:
+                nc.vector.tensor_copy(out=dgT_j[:], in_=dg_bank[:])
+            else:
+                nc.scalar.copy(out=dgT_j[:], in_=dg_bank[:])
+            dgT.append(dgT_j)
+
+        out_banks = []
+        for t in range(ROW_TILES):
+            out_bank = banks.tile([P, GROUPS * COEFFS], F32, tag="bank", name="out_bank%d" % t)
+            out_banks.append(out_bank)
+
+        def second_matmul(t, j):
+            cols = slice(j * COEFFS, (j + 1) * COEFFS)
+            nc.tensor.matmul(
+                out=out_banks[t][:, cols], lhsT=dgT[j][:, t * P : (t + 1) * P], rhs=k2T[:, cols], start=True, stop=True
+            )
+
+        for t in range(ROW_TILES):
+            second_matmul(t, 0)
+        for t in range(ROW_TILES):
+            for j in range(1, GROUPS):
+                second_matmul(t, j)
+            out_sb = keep.tile([P, GROUPS * COEFFS], F32, name="out_sb%d" % t)
+            if t % 2 == 0:
+                nc.vector.tensor_copy(out=out_sb[:], in_=out_banks[t][:])
+            else:
+                nc.scalar.copy(out=out_sb[:], in_=out_banks[t][:])
+            nc.sync.dma_start(out=out_rows[:, t, :], in_=out_sb[:])

@@ -19,6 +19,7 @@ ROW_TILES = SAMPLES // P
 WORDS = WINDOW // 2
 HALVES = WORDS // P
 PACK = 4
+PAIR = 2
 
 FLOPS = 2 * SAMPLES * WINDOW * GROUPS * COEFFS + 2 * SAMPLES * GROUPS * COEFFS * COEFFS
 BYTES = 2 * (SAMPLES * WINDOW + GROUPS * COEFFS * WINDOW + GROUPS * COEFFS * COEFFS) + 4 * SAMPLES * GROUPS * COEFFS
@@ -29,124 +30,121 @@ def transpose_row_tile(nc, bank, words, identity):
         nc.tensor.transpose(out=bank[:, u, :], in_=words[:, u * P : (u + 1) * P], identity=identity)
 
 
+def leave_psum(nc, index, sbuf, psum):
+    if index % 2 == 0:
+        nc.vector.tensor_copy(out=sbuf, in_=psum)
+    else:
+        nc.scalar.copy(out=sbuf, in_=psum)
+
+
 def tile_switchnet_fstar_pb_s_kernel(tc, h_switch, k2, b2, k3, b3, grad_out, out):
     nc = tc.nc
     with ExitStack() as ctx:
         keep = ctx.enter_context(tc.tile_pool(name="keep", bufs=1))
         banks = ctx.enter_context(tc.psum_pool(name="banks", bufs=8))
 
-        dy_rows = grad_out.rearrange("(p t) x y c -> p t (x y c)", t=ROW_TILES)
-        k3_rows = k3.rearrange("o (j p) l -> p (o j) l", p=P)
-        k2_rows = k2.rearrange("j (q t) r -> (j q) (t r)", t=GROUPS)
-        out_rows = out.rearrange("(p t) j r -> p t (j r)", t=ROW_TILES)
+        with tc.manual_schedule():
+            dy_rows = grad_out.rearrange("(p t) x y c -> p t (x y c)", t=ROW_TILES)
+            k3_rows = k3.rearrange("o (j p) l -> p (o j) l", p=P)
+            k2_rows = k2.rearrange("j (q t) r -> (j q) (t r)", t=GROUPS)
+            out_rows = out.rearrange("(p t) j r -> p t (j r)", t=ROW_TILES)
 
-        dy_sb = keep.tile([P, ROW_TILES * WINDOW], BF16)
-        k3_sb = keep.tile([P, GROUPS * WINDOW], BF16)
-        k2_sb = keep.tile([P, GROUPS * COEFFS], BF16)
-        dy_sb_tiles = dy_sb[:].rearrange("p (t l) -> p t l", t=ROW_TILES)
-        for h in range(2):
-            nc.sync.dma_start(out=dy_sb_tiles[:, 2 * h : 2 * h + 2, :], in_=dy_rows[:, 2 * h : 2 * h + 2, :])
-        nc.sync.dma_start(out=k3_sb[:, 0:WINDOW], in_=k3_rows[:, 0, :])
-        nc.sync.dma_start(out=k2_sb[:], in_=k2_rows)
-        for j in range(1, GROUPS):
-            nc.sync.dma_start(out=k3_sb[:, j * WINDOW : (j + 1) * WINDOW], in_=k3_rows[:, j, :])
+            dy_sb = keep.tile([P, ROW_TILES * WINDOW], BF16)
+            k3_sb = keep.tile([P, GROUPS * WINDOW], BF16)
+            k2_sb = keep.tile([P, GROUPS * COEFFS], BF16)
+            dy_sb_tiles = dy_sb[:].rearrange("p (t l) -> p t l", t=ROW_TILES)
+            for h in range(ROW_TILES // PAIR):
+                tiles = slice(PAIR * h, PAIR * (h + 1))
+                nc.sync.dma_start(out=dy_sb_tiles[:, tiles, :], in_=dy_rows[:, tiles, :])
+            for j in range(GROUPS):
+                nc.sync.dma_start(out=k3_sb[:, j * WINDOW : (j + 1) * WINDOW], in_=k3_rows[:, j, :])
+            nc.sync.dma_start(out=k2_sb[:], in_=k2_rows)
 
-        identity_f32 = keep.tile([P, P], F32)
-        make_identity(nc, identity_f32[:])
-        identity_bf16 = keep.tile([P, P], BF16)
-        nc.vector.tensor_copy(out=identity_bf16[:], in_=identity_f32[:])
+            identity_f32 = keep.tile([P, P], F32)
+            make_identity(nc, identity_f32[:])
+            identity_bf16 = keep.tile([P, P], BF16)
+            nc.vector.tensor_copy(out=identity_bf16[:], in_=identity_f32[:])
 
-        dy_words = dy_sb[:].bitcast(F32)
-        dy_grouped = keep.tile([P, SAMPLES * PACK], BF16, align_bytes=64)
-        dy_grouped_words = dy_grouped[:].bitcast(F32)
-        dy_codes = keep.tile([P, SAMPLES], U32, align_bytes=64)
-        dy_scales = keep.tile([P, SAMPLES], U8, align_bytes=64)
-        for h in range(2):
-            dy_bank = banks.tile([P, 2, HALVES, P], F32, tag="bank")
-            for t in range(2):
-                first_word = (2 * h + t) * WORDS
-                transpose_row_tile(nc, dy_bank[:, t], dy_words[:, first_word : first_word + WORDS], identity_f32[:])
-            nc.scalar.copy(
-                out=dy_grouped_words[:, 2 * h * WORDS : (2 * h + 2) * WORDS].rearrange(
-                    "p (t r u) -> p t r u", t=2, u=HALVES
-                ),
-                in_=dy_bank[:].rearrange("p t u r -> p t r u"),
-            )
-            cols = slice(2 * h * P, (2 * h + 2) * P)
-            nc.vector.quantize_mx(
-                out=dy_codes[:, cols].bitcast(E5M2_X4),
-                scales=dy_scales[:, cols],
-                in_=dy_grouped[:, 2 * h * P * PACK : (2 * h + 2) * P * PACK],
-            )
-
-        k3_words = k3_sb[:].bitcast(F32)
-        k3_grouped = keep.tile([P, GROUPS * COEFFS * PACK], BF16, align_bytes=64)
-        k3_grouped_words = k3_grouped[:].bitcast(F32)
-        k3_codes = keep.tile([P, GROUPS * COEFFS], U32, align_bytes=64)
-        k3_scales = keep.tile([P, GROUPS * COEFFS], U8, align_bytes=64)
-        k2T = keep.tile([P, GROUPS * COEFFS], F32)
-        for j in range(GROUPS):
-            k3_bank = banks.tile([P, HALVES, P], F32, tag="bank")
-            transpose_row_tile(nc, k3_bank, k3_words[:, j * WORDS : (j + 1) * WORDS], identity_f32[:])
-            nc.scalar.copy(
-                out=k3_grouped_words[:, j * WORDS : (j + 1) * WORDS].rearrange("p (r u) -> p r u", u=HALVES),
-                in_=k3_bank[:].rearrange("p u r -> p r u"),
-            )
-            cols = slice(j * COEFFS, (j + 1) * COEFFS)
-            nc.vector.quantize_mx(
-                out=k3_codes[:, cols].bitcast(E4M3_X4),
-                scales=k3_scales[:, cols],
-                in_=k3_grouped[:, j * COEFFS * PACK : (j + 1) * COEFFS * PACK],
-            )
-            if j == 0:
-                k2_bank = banks.tile([P, GROUPS, P], BF16, tag="bank")
-                for t in range(GROUPS):
-                    nc.tensor.transpose(
-                        out=k2_bank[:, t, :], in_=k2_sb[:, t * COEFFS : (t + 1) * COEFFS], identity=identity_bf16[:]
-                    )
+            dy_words = dy_sb[:].bitcast(F32)
+            dy_grouped = keep.tile([P, SAMPLES * PACK], BF16, align_bytes=64)
+            dy_grouped_words = dy_grouped[:].bitcast(F32)
+            dy_codes = keep.tile([P, SAMPLES], U32, align_bytes=64)
+            dy_scales = keep.tile([P, SAMPLES], U8, align_bytes=64)
+            for h in range(ROW_TILES // PAIR):
+                dy_bank = banks.tile([P, PAIR, HALVES, P], F32, tag="bank")
+                for t in range(PAIR):
+                    first_word = (PAIR * h + t) * WORDS
+                    transpose_row_tile(nc, dy_bank[:, t], dy_words[:, first_word : first_word + WORDS], identity_f32[:])
                 nc.scalar.copy(
-                    out=k2T[:].rearrange("r (p t) -> r p t", t=GROUPS), in_=k2_bank[:].rearrange("r t p -> r p t")
+                    out=dy_grouped_words[:, PAIR * h * WORDS : PAIR * (h + 1) * WORDS].rearrange(
+                        "p (t r u) -> p t r u", t=PAIR, u=HALVES
+                    ),
+                    in_=dy_bank[:].rearrange("p t u r -> p t r u"),
+                )
+                cols = slice(PAIR * h * P, PAIR * (h + 1) * P)
+                nc.vector.quantize_mx(
+                    out=dy_codes[:, cols].bitcast(E5M2_X4),
+                    scales=dy_scales[:, cols],
+                    in_=dy_grouped[:, PAIR * h * P * PACK : PAIR * (h + 1) * P * PACK],
                 )
 
-        dgT = []
-        for j in range(GROUPS):
-            cols = slice(j * COEFFS, (j + 1) * COEFFS)
-            dg_bank = banks.tile([P, SAMPLES], F32, tag="bank")
-            nc.tensor.matmul_mx(
-                out=dg_bank[:],
-                lhsT=k3_codes[:, cols].bitcast(E4M3_X4),
-                lhsT_scale=k3_scales[:, cols],
-                rhs=dy_codes[:].bitcast(E5M2_X4),
-                rhs_scale=dy_scales[:],
-                start=True,
-                stop=True,
-            )
-            dgT_j = keep.tile([P, SAMPLES], F32, name="dgT%d" % j)
-            if j % 2 == 0:
-                nc.vector.tensor_copy(out=dgT_j[:], in_=dg_bank[:])
-            else:
-                nc.scalar.copy(out=dgT_j[:], in_=dg_bank[:])
-            dgT.append(dgT_j)
+            k3_words = k3_sb[:].bitcast(F32)
+            k3_grouped = keep.tile([P, GROUPS * COEFFS * PACK], BF16, align_bytes=64)
+            k3_grouped_words = k3_grouped[:].bitcast(F32)
+            k3_codes = keep.tile([P, GROUPS * COEFFS], U32, align_bytes=64)
+            k3_scales = keep.tile([P, GROUPS * COEFFS], U8, align_bytes=64)
+            for j in range(GROUPS):
+                k3_bank = banks.tile([P, HALVES, P], F32, tag="bank")
+                transpose_row_tile(nc, k3_bank, k3_words[:, j * WORDS : (j + 1) * WORDS], identity_f32[:])
+                nc.scalar.copy(
+                    out=k3_grouped_words[:, j * WORDS : (j + 1) * WORDS].rearrange("p (r u) -> p r u", u=HALVES),
+                    in_=k3_bank[:].rearrange("p u r -> p r u"),
+                )
+                cols = slice(j * COEFFS, (j + 1) * COEFFS)
+                nc.vector.quantize_mx(
+                    out=k3_codes[:, cols].bitcast(E4M3_X4),
+                    scales=k3_scales[:, cols],
+                    in_=k3_grouped[:, j * COEFFS * PACK : (j + 1) * COEFFS * PACK],
+                )
 
-        out_banks = []
-        for t in range(ROW_TILES):
-            out_bank = banks.tile([P, GROUPS * COEFFS], F32, tag="bank", name="out_bank%d" % t)
-            out_banks.append(out_bank)
+            k2T = keep.tile([P, GROUPS * COEFFS], F32)
+            k2_bank = banks.tile([P, GROUPS, P], BF16, tag="bank")
+            for t in range(GROUPS):
+                nc.tensor.transpose(
+                    out=k2_bank[:, t, :], in_=k2_sb[:, t * COEFFS : (t + 1) * COEFFS], identity=identity_bf16[:]
+                )
+            nc.scalar.copy(out=k2T[:].rearrange("r (p t) -> r p t", t=GROUPS), in_=k2_bank[:].rearrange("r t p -> r p t"))
 
-        def second_matmul(t, j):
-            cols = slice(j * COEFFS, (j + 1) * COEFFS)
-            nc.tensor.matmul(
-                out=out_banks[t][:, cols], lhsT=dgT[j][:, t * P : (t + 1) * P], rhs=k2T[:, cols], start=True, stop=True
-            )
+            dgT = []
+            for j in range(GROUPS):
+                cols = slice(j * COEFFS, (j + 1) * COEFFS)
+                dg_bank = banks.tile([P, SAMPLES], F32, tag="bank")
+                nc.tensor.matmul_mx(
+                    out=dg_bank[:],
+                    lhsT=k3_codes[:, cols].bitcast(E4M3_X4),
+                    lhsT_scale=k3_scales[:, cols],
+                    rhs=dy_codes[:].bitcast(E5M2_X4),
+                    rhs_scale=dy_scales[:],
+                    start=True,
+                    stop=True,
+                )
+                dgT_j = keep.tile([P, SAMPLES], F32, name="dgT%d" % j)
+                for half in (slice(0, SAMPLES // 2), slice(SAMPLES // 2, SAMPLES)):
+                    leave_psum(nc, j, dgT_j[:, half], dg_bank[:, half])
+                dgT.append(dgT_j)
 
-        for t in range(ROW_TILES):
-            second_matmul(t, 0)
-        for t in range(ROW_TILES):
-            for j in range(1, GROUPS):
-                second_matmul(t, j)
-            out_sb = keep.tile([P, GROUPS * COEFFS], F32, name="out_sb%d" % t)
-            if t % 2 == 0:
-                nc.vector.tensor_copy(out=out_sb[:], in_=out_banks[t][:])
-            else:
-                nc.scalar.copy(out=out_sb[:], in_=out_banks[t][:])
-            nc.sync.dma_start(out=out_rows[:, t, :], in_=out_sb[:])
+            for t in range(ROW_TILES):
+                for pair in range(GROUPS // PAIR):
+                    out_bank = banks.tile([P, PAIR, COEFFS], F32, tag="bank")
+                    for i in range(PAIR):
+                        j = PAIR * pair + i
+                        nc.tensor.matmul(
+                            out=out_bank[:, i, :],
+                            lhsT=dgT[j][:, t * P : (t + 1) * P],
+                            rhs=k2T[:, j * COEFFS : (j + 1) * COEFFS],
+                            start=True,
+                            stop=True,
+                        )
+                    out_sb = keep.tile([P, PAIR * COEFFS], F32, name="out_sb%d%d" % (t, pair))
+                    leave_psum(nc, pair, out_sb[:], out_bank[:].rearrange("p i r -> p (i r)"))
+                    nc.sync.dma_start(out=out_rows[:, t, pair * PAIR * COEFFS : (pair + 1) * PAIR * COEFFS], in_=out_sb[:])

@@ -7,6 +7,7 @@ F32 = mybir.dt.float32
 BF16 = mybir.dt.bfloat16
 U32 = mybir.dt.uint32
 U8 = mybir.dt.uint8
+I32 = mybir.dt.int32
 E4M3_X4 = mybir.dt.float8_e4m3fn_x4
 E5M2_X4 = mybir.dt.float8_e5m2_x4
 
@@ -19,6 +20,8 @@ ROW_TILES = SAMPLES // P
 WORDS = WINDOW // 2
 HALVES = WORDS // P
 PACK = 4
+HEAD_MATMULS = 3
+MID_PASSES = 2
 PAIR = 2
 
 FLOPS = 2 * SAMPLES * WINDOW * GROUPS * COEFFS + 2 * SAMPLES * GROUPS * COEFFS * COEFFS
@@ -65,6 +68,20 @@ def tile_switchnet_fstar_pb_s_kernel(tc, h_switch, k2, b2, k3, b3, grad_out, out
             identity_bf16 = keep.tile([P, P], BF16)
             nc.vector.tensor_copy(out=identity_bf16[:], in_=identity_f32[:])
 
+            idle_bank = banks.tile([P, SAMPLES], F32, tag="bank")
+            for i in range(HEAD_MATMULS):
+                nc.tensor.matmul(out=idle_bank[:, 0:P], lhsT=identity_f32[:], rhs=identity_f32[:], start=True, stop=True)
+            zeros = keep.tile([P, SAMPLES * PACK], BF16, align_bytes=64)
+            zero_moving = keep.tile([P, SAMPLES], U32, align_bytes=64)
+            zero_moving_scales = keep.tile([P, SAMPLES], U8, align_bytes=64)
+            zero_stationary = keep.tile([P, P], U32, align_bytes=64)
+            zero_stationary_scales = keep.tile([P, P], U8, align_bytes=64)
+            nc.vector.memset(zeros[:].bitcast(I32), 0)
+            nc.vector.quantize_mx(out=zero_moving[:].bitcast(E5M2_X4), scales=zero_moving_scales[:], in_=zeros[:])
+            nc.vector.quantize_mx(
+                out=zero_stationary[:].bitcast(E4M3_X4), scales=zero_stationary_scales[:], in_=zeros[:, 0 : P * PACK]
+            )
+
             dy_words = dy_sb[:].bitcast(F32)
             dy_grouped = keep.tile([P, SAMPLES * PACK], BF16, align_bytes=64)
             dy_grouped_words = dy_grouped[:].bitcast(F32)
@@ -106,6 +123,17 @@ def tile_switchnet_fstar_pb_s_kernel(tc, h_switch, k2, b2, k3, b3, grad_out, out
                     scales=k3_scales[:, cols],
                     in_=k3_grouped[:, j * COEFFS * PACK : (j + 1) * COEFFS * PACK],
                 )
+                if j == 0:
+                    for i in range(MID_PASSES):
+                        nc.tensor.matmul_mx(
+                            out=idle_bank[:],
+                            lhsT=zero_stationary[:].bitcast(E4M3_X4),
+                            lhsT_scale=zero_stationary_scales[:],
+                            rhs=zero_moving[:].bitcast(E5M2_X4),
+                            rhs_scale=zero_moving_scales[:],
+                            start=True,
+                            stop=True,
+                        )
 
             k2T = keep.tile([P, GROUPS * COEFFS], F32)
             k2_bank = banks.tile([P, GROUPS, P], BF16, tag="bank")

@@ -33,15 +33,10 @@ def transpose_row_tile(nc, bank, words, identity):
         nc.tensor.transpose(out=bank[:, u, :], in_=words[:, u * P : (u + 1) * P], identity=identity)
 
 
-def leave_psum(nc, index, sbuf, psum):
-    if index % 2 == 0:
-        nc.vector.tensor_copy(out=sbuf, in_=psum)
-    else:
-        nc.scalar.copy(out=sbuf, in_=psum)
-
-
 def tile_switchnet_fstar_pb_s_kernel(tc, h_switch, k2, b2, k3, b3, grad_out, out):
     nc = tc.nc
+    on_vector = nc.vector.tensor_copy
+    on_scalar = nc.scalar.copy
     with ExitStack() as ctx:
         keep = ctx.enter_context(tc.tile_pool(name="keep", bufs=1))
         banks = ctx.enter_context(tc.psum_pool(name="banks", bufs=8))
@@ -60,8 +55,9 @@ def tile_switchnet_fstar_pb_s_kernel(tc, h_switch, k2, b2, k3, b3, grad_out, out
                 tiles = slice(PAIR * h, PAIR * (h + 1))
                 nc.sync.dma_start(out=dy_sb_tiles[:, tiles, :], in_=dy_rows[:, tiles, :])
             for j in range(GROUPS):
+                if j == 2:
+                    nc.sync.dma_start(out=k2_sb[:], in_=k2_rows)
                 nc.sync.dma_start(out=k3_sb[:, j * WINDOW : (j + 1) * WINDOW], in_=k3_rows[:, j, :])
-            nc.sync.dma_start(out=k2_sb[:], in_=k2_rows)
 
             identity_f32 = keep.tile([P, P], F32)
             make_identity(nc, identity_f32[:])
@@ -87,68 +83,40 @@ def tile_switchnet_fstar_pb_s_kernel(tc, h_switch, k2, b2, k3, b3, grad_out, out
             dy_grouped_words = dy_grouped[:].bitcast(F32)
             dy_codes = keep.tile([P, SAMPLES], U32, align_bytes=64)
             dy_scales = keep.tile([P, SAMPLES], U8, align_bytes=64)
-            for h in range(ROW_TILES // PAIR):
-                dy_bank = banks.tile([P, PAIR, HALVES, P], F32, tag="bank")
-                for t in range(PAIR):
-                    first_word = (PAIR * h + t) * WORDS
-                    transpose_row_tile(nc, dy_bank[:, t], dy_words[:, first_word : first_word + WORDS], identity_f32[:])
-                nc.scalar.copy(
-                    out=dy_grouped_words[:, PAIR * h * WORDS : PAIR * (h + 1) * WORDS].rearrange(
-                        "p (t r u) -> p t r u", t=PAIR, u=HALVES
-                    ),
-                    in_=dy_bank[:].rearrange("p t u r -> p t r u"),
-                )
-                cols = slice(PAIR * h * P, PAIR * (h + 1) * P)
-                nc.vector.quantize_mx(
-                    out=dy_codes[:, cols].bitcast(E5M2_X4),
-                    scales=dy_scales[:, cols],
-                    in_=dy_grouped[:, PAIR * h * P * PACK : PAIR * (h + 1) * P * PACK],
-                )
-
             k3_words = k3_sb[:].bitcast(F32)
             k3_grouped = keep.tile([P, GROUPS * COEFFS * PACK], BF16, align_bytes=64)
             k3_grouped_words = k3_grouped[:].bitcast(F32)
             k3_codes = keep.tile([P, GROUPS * COEFFS], U32, align_bytes=64)
             k3_scales = keep.tile([P, GROUPS * COEFFS], U8, align_bytes=64)
-            for j in range(GROUPS):
-                k3_bank = banks.tile([P, HALVES, P], F32, tag="bank")
-                transpose_row_tile(nc, k3_bank, k3_words[:, j * WORDS : (j + 1) * WORDS], identity_f32[:])
-                nc.scalar.copy(
-                    out=k3_grouped_words[:, j * WORDS : (j + 1) * WORDS].rearrange("p (r u) -> p r u", u=HALVES),
-                    in_=k3_bank[:].rearrange("p u r -> p r u"),
-                )
-                cols = slice(j * COEFFS, (j + 1) * COEFFS)
-                nc.vector.quantize_mx(
-                    out=k3_codes[:, cols].bitcast(E4M3_X4),
-                    scales=k3_scales[:, cols],
-                    in_=k3_grouped[:, j * COEFFS * PACK : (j + 1) * COEFFS * PACK],
-                )
-                if j == 0:
-                    for i in range(MID_PASSES):
-                        nc.tensor.matmul_mx(
-                            out=idle_bank[:],
-                            lhsT=zero_stationary[:].bitcast(E4M3_X4),
-                            lhsT_scale=zero_stationary_scales[:],
-                            rhs=zero_moving[:].bitcast(E5M2_X4),
-                            rhs_scale=zero_moving_scales[:],
-                            start=True,
-                            stop=True,
-                        )
-
             k2T = keep.tile([P, GROUPS * COEFFS], F32)
-            k2_bank = banks.tile([P, GROUPS, P], BF16, tag="bank")
-            for t in range(GROUPS):
-                nc.tensor.transpose(
-                    out=k2_bank[:, t, :], in_=k2_sb[:, t * COEFFS : (t + 1) * COEFFS], identity=identity_bf16[:]
-                )
-            nc.scalar.copy(out=k2T[:].rearrange("r (p t) -> r p t", t=GROUPS), in_=k2_bank[:].rearrange("r t p -> r p t"))
+            dgT = [keep.tile([P, SAMPLES], F32, name="dgT%d" % j) for j in range(GROUPS)]
 
-            dgT = []
-            for j in range(GROUPS):
+            def transpose_and_group(words, grouped_words, first, count, engine_copy):
+                bank = banks.tile([P, count, HALVES, P], F32, tag="bank", name="t_bank")
+                for i in range(count):
+                    transpose_row_tile(
+                        nc, bank[:, i], words[:, (first + i) * WORDS : (first + i + 1) * WORDS], identity_f32[:]
+                    )
+                engine_copy(
+                    out=grouped_words[:, first * WORDS : (first + count) * WORDS].rearrange(
+                        "p (t r u) -> p t r u", t=count, u=HALVES
+                    ),
+                    in_=bank[:].rearrange("p t u r -> p t r u"),
+                )
+
+            def quantise(codes, scales, grouped, fmt, first, count):
+                cols = slice(first * P, (first + count) * P)
+                nc.vector.quantize_mx(
+                    out=codes[:, cols].bitcast(fmt),
+                    scales=scales[:, cols],
+                    in_=grouped[:, first * P * PACK : (first + count) * P * PACK],
+                )
+
+            def mx_pass(j):
                 cols = slice(j * COEFFS, (j + 1) * COEFFS)
-                dg_bank = banks.tile([P, SAMPLES], F32, tag="bank")
+                bank = banks.tile([P, SAMPLES], F32, tag="bank", name="dg_bank")
                 nc.tensor.matmul_mx(
-                    out=dg_bank[:],
+                    out=bank[:],
                     lhsT=k3_codes[:, cols].bitcast(E4M3_X4),
                     lhsT_scale=k3_scales[:, cols],
                     rhs=dy_codes[:].bitcast(E5M2_X4),
@@ -156,23 +124,83 @@ def tile_switchnet_fstar_pb_s_kernel(tc, h_switch, k2, b2, k3, b3, grad_out, out
                     start=True,
                     stop=True,
                 )
-                dgT_j = keep.tile([P, SAMPLES], F32, name="dgT%d" % j)
-                for half in (slice(0, SAMPLES // 2), slice(SAMPLES // 2, SAMPLES)):
-                    leave_psum(nc, j, dgT_j[:, half], dg_bank[:, half])
-                dgT.append(dgT_j)
+                return bank
 
-            for t in range(ROW_TILES):
-                for pair in range(GROUPS // PAIR):
-                    out_bank = banks.tile([P, PAIR, COEFFS], F32, tag="bank")
-                    for i in range(PAIR):
-                        j = PAIR * pair + i
-                        nc.tensor.matmul(
-                            out=out_bank[:, i, :],
-                            lhsT=dgT[j][:, t * P : (t + 1) * P],
-                            rhs=k2T[:, j * COEFFS : (j + 1) * COEFFS],
-                            start=True,
-                            stop=True,
-                        )
-                    out_sb = keep.tile([P, PAIR * COEFFS], F32, name="out_sb%d%d" % (t, pair))
-                    leave_psum(nc, pair, out_sb[:], out_bank[:].rearrange("p i r -> p (i r)"))
-                    nc.sync.dma_start(out=out_rows[:, t, pair * PAIR * COEFFS : (pair + 1) * PAIR * COEFFS], in_=out_sb[:])
+            def leave(j, bank, first, count, engine_copy):
+                cols = slice(first * P, (first + count) * P)
+                engine_copy(out=dgT[j][:, cols], in_=bank[:, cols])
+
+            def second(dst, j, t):
+                nc.tensor.matmul(
+                    out=dst,
+                    lhsT=dgT[j][:, t * P : (t + 1) * P],
+                    rhs=k2T[:, j * COEFFS : (j + 1) * COEFFS],
+                    start=True,
+                    stop=True,
+                )
+
+            transpose_and_group(dy_words, dy_grouped_words, 0, 2, on_scalar)
+            transpose_and_group(dy_words, dy_grouped_words, 2, 2, on_vector)
+            quantise(dy_codes, dy_scales, dy_grouped, E5M2_X4, 0, 2)
+            quantise(dy_codes, dy_scales, dy_grouped, E5M2_X4, 2, 2)
+            transpose_and_group(k3_words, k3_grouped_words, 0, 1, on_scalar)
+            quantise(k3_codes, k3_scales, k3_grouped, E4M3_X4, 0, 1)
+            for i in range(MID_PASSES):
+                nc.tensor.matmul_mx(
+                    out=idle_bank[:],
+                    lhsT=zero_stationary[:].bitcast(E4M3_X4),
+                    lhsT_scale=zero_stationary_scales[:],
+                    rhs=zero_moving[:].bitcast(E5M2_X4),
+                    rhs_scale=zero_moving_scales[:],
+                    start=True,
+                    stop=True,
+                )
+            transpose_and_group(k3_words, k3_grouped_words, 1, 1, on_scalar)
+            quantise(k3_codes, k3_scales, k3_grouped, E4M3_X4, 1, 1)
+            k2_bank = banks.tile([P, GROUPS, P], BF16, tag="bank")
+            for t in range(GROUPS):
+                nc.tensor.transpose(
+                    out=k2_bank[:, t, :], in_=k2_sb[:, t * COEFFS : (t + 1) * COEFFS], identity=identity_bf16[:]
+                )
+            nc.scalar.copy(out=k2T[:].rearrange("r (p t) -> r p t", t=GROUPS), in_=k2_bank[:].rearrange("r t p -> r p t"))
+            transpose_and_group(k3_words, k3_grouped_words, 2, 1, on_vector)
+            transpose_and_group(k3_words, k3_grouped_words, 3, 1, on_scalar)
+
+            dg = [mx_pass(0), mx_pass(1)]
+            leave(0, dg[0], 0, 2, on_vector)
+            leave(1, dg[1], 0, 2, on_scalar)
+            quantise(k3_codes, k3_scales, k3_grouped, E4M3_X4, 2, 1)
+            leave(0, dg[0], 2, 2, on_vector)
+            leave(1, dg[1], 2, 2, on_scalar)
+            quantise(k3_codes, k3_scales, k3_grouped, E4M3_X4, 3, 1)
+
+            def out_pair(first, t):
+                bank = banks.tile([P, 2, COEFFS], F32, tag="bank", name="out_bank")
+                sb = keep.tile([P, 2, COEFFS], F32, name="out_sb%d%d" % (first, t))
+                for i in range(2):
+                    second(bank[:, i, :], first + i, t)
+                copy = on_vector if t % 2 == 0 else on_scalar
+                copy(out=sb[:], in_=bank[:])
+                nc.sync.dma_start(
+                    out=out_rows[:, t, first * COEFFS : (first + 2) * COEFFS], in_=sb[:].rearrange("p i r -> p (i r)")
+                )
+
+            out_pair(0, 0)
+            out_pair(0, 1)
+            dg.append(mx_pass(2))
+            dg.append(mx_pass(3))
+            for c in range(2):
+                leave(2, dg[2], 2 * c, 2, on_vector)
+                leave(3, dg[3], 2 * c, 2, on_scalar)
+            out_pair(0, 2)
+            out_pair(0, 3)
+            for t in range(ROW_TILES - 1):
+                out_pair(2, t)
+            t = ROW_TILES - 1
+            for i in range(2):
+                bank = banks.tile([P, COEFFS], F32, tag="bank", name="end_bank")
+                sb = keep.tile([P, COEFFS], F32, name="end_sb%d" % i)
+                second(bank[:], 2 + i, t)
+                copy = on_scalar if i == 0 else on_vector
+                copy(out=sb[:], in_=bank[:])
+                nc.sync.dma_start(out=out_rows[:, t, (2 + i) * COEFFS : (3 + i) * COEFFS], in_=sb[:])

@@ -55,9 +55,8 @@ def tile_switchnet_fstar_pb_s_kernel(tc, h_switch, k2, b2, k3, b3, grad_out, out
                 tiles = slice(PAIR * h, PAIR * (h + 1))
                 nc.sync.dma_start(out=dy_sb_tiles[:, tiles, :], in_=dy_rows[:, tiles, :])
             for j in range(GROUPS):
-                if j == 2:
-                    nc.sync.dma_start(out=k2_sb[:], in_=k2_rows)
                 nc.sync.dma_start(out=k3_sb[:, j * WINDOW : (j + 1) * WINDOW], in_=k3_rows[:, j, :])
+            nc.sync.dma_start(out=k2_sb[:], in_=k2_rows)
 
             identity_f32 = keep.tile([P, P], F32)
             make_identity(nc, identity_f32[:])
@@ -155,52 +154,31 @@ def tile_switchnet_fstar_pb_s_kernel(tc, h_switch, k2, b2, k3, b3, grad_out, out
                     start=True,
                     stop=True,
                 )
-            transpose_and_group(k3_words, k3_grouped_words, 1, 1, on_scalar)
-            quantise(k3_codes, k3_scales, k3_grouped, E4M3_X4, 1, 1)
+            for j in range(1, GROUPS):
+                transpose_and_group(k3_words, k3_grouped_words, j, 1, on_vector if j == 2 else on_scalar)
+            for j in range(1, GROUPS):
+                quantise(k3_codes, k3_scales, k3_grouped, E4M3_X4, j, 1)
             k2_bank = banks.tile([P, GROUPS, P], BF16, tag="bank")
             for t in range(GROUPS):
                 nc.tensor.transpose(
                     out=k2_bank[:, t, :], in_=k2_sb[:, t * COEFFS : (t + 1) * COEFFS], identity=identity_bf16[:]
                 )
             nc.scalar.copy(out=k2T[:].rearrange("r (p t) -> r p t", t=GROUPS), in_=k2_bank[:].rearrange("r t p -> r p t"))
-            transpose_and_group(k3_words, k3_grouped_words, 2, 1, on_vector)
-            transpose_and_group(k3_words, k3_grouped_words, 3, 1, on_scalar)
 
-            dg = [mx_pass(0), mx_pass(1)]
-            leave(0, dg[0], 0, 2, on_vector)
-            leave(1, dg[1], 0, 2, on_scalar)
-            quantise(k3_codes, k3_scales, k3_grouped, E4M3_X4, 2, 1)
-            leave(0, dg[0], 2, 2, on_vector)
-            leave(1, dg[1], 2, 2, on_scalar)
-            quantise(k3_codes, k3_scales, k3_grouped, E4M3_X4, 3, 1)
+            dg = [mx_pass(j) for j in range(GROUPS)]
+            for first in range(0, GROUPS, 2):
+                for half in range(2):
+                    leave(first, dg[first], 2 * half, 2, on_vector)
+                    leave(first + 1, dg[first + 1], 2 * half, 2, on_scalar)
 
-            def out_pair(first, t):
-                bank = banks.tile([P, 2, COEFFS], F32, tag="bank", name="out_bank")
-                sb = keep.tile([P, 2, COEFFS], F32, name="out_sb%d%d" % (first, t))
-                for i in range(2):
-                    second(bank[:, i, :], first + i, t)
-                copy = on_vector if t % 2 == 0 else on_scalar
-                copy(out=sb[:], in_=bank[:])
-                nc.sync.dma_start(
-                    out=out_rows[:, t, first * COEFFS : (first + 2) * COEFFS], in_=sb[:].rearrange("p i r -> p (i r)")
-                )
-
-            out_pair(0, 0)
-            out_pair(0, 1)
-            dg.append(mx_pass(2))
-            dg.append(mx_pass(3))
-            for c in range(2):
-                leave(2, dg[2], 2 * c, 2, on_vector)
-                leave(3, dg[3], 2 * c, 2, on_scalar)
-            out_pair(0, 2)
-            out_pair(0, 3)
-            for t in range(ROW_TILES - 1):
-                out_pair(2, t)
-            t = ROW_TILES - 1
-            for i in range(2):
-                bank = banks.tile([P, COEFFS], F32, tag="bank", name="end_bank")
-                sb = keep.tile([P, COEFFS], F32, name="end_sb%d" % i)
-                second(bank[:], 2 + i, t)
-                copy = on_scalar if i == 0 else on_vector
-                copy(out=sb[:], in_=bank[:])
-                nc.sync.dma_start(out=out_rows[:, t, (2 + i) * COEFFS : (3 + i) * COEFFS], in_=sb[:])
+            for first in range(0, GROUPS, 2):
+                for t in range(ROW_TILES):
+                    bank = banks.tile([P, 2, COEFFS], F32, tag="bank", name="out_bank")
+                    sb = keep.tile([P, 2, COEFFS], F32, name="out_sb%d%d" % (first, t))
+                    for i in range(2):
+                        second(bank[:, i, :], first + i, t)
+                    copy = on_vector if t % 2 == 0 else on_scalar
+                    copy(out=sb[:], in_=bank[:])
+                    nc.sync.dma_start(
+                        out=out_rows[:, t, first * COEFFS : (first + 2) * COEFFS], in_=sb[:].rearrange("p i r -> p (i r)")
+                    )

@@ -139,7 +139,7 @@ def tile_switchnet_fstar_pb_s_kernel(tc, h_switch, k2, b2, k3, b3, grad_out, out
                 )
 
             transpose_and_group(dy_words, dy_grouped_words, 0, 2, on_scalar)
-            transpose_and_group(dy_words, dy_grouped_words, 2, 2, on_vector)
+            transpose_and_group(dy_words, dy_grouped_words, 2, 2, on_scalar)
             quantise(dy_codes, dy_scales, dy_grouped, E5M2_X4, 0, 2)
             quantise(dy_codes, dy_scales, dy_grouped, E5M2_X4, 2, 2)
             transpose_and_group(k3_words, k3_grouped_words, 0, 1, on_scalar)
@@ -155,8 +155,7 @@ def tile_switchnet_fstar_pb_s_kernel(tc, h_switch, k2, b2, k3, b3, grad_out, out
                     stop=True,
                 )
             for j in range(1, GROUPS):
-                transpose_and_group(k3_words, k3_grouped_words, j, 1, on_vector if j == 2 else on_scalar)
-            for j in range(1, GROUPS):
+                transpose_and_group(k3_words, k3_grouped_words, j, 1, on_scalar)
                 quantise(k3_codes, k3_scales, k3_grouped, E4M3_X4, j, 1)
             k2_bank = banks.tile([P, GROUPS, P], BF16, tag="bank")
             for t in range(GROUPS):
@@ -173,12 +172,18 @@ def tile_switchnet_fstar_pb_s_kernel(tc, h_switch, k2, b2, k3, b3, grad_out, out
 
             for first in range(0, GROUPS, 2):
                 for t in range(ROW_TILES):
-                    bank = banks.tile([P, 2, COEFFS], F32, tag="bank", name="out_bank")
                     sb = keep.tile([P, 2, COEFFS], F32, name="out_sb%d%d" % (first, t))
-                    for i in range(2):
-                        second(bank[:, i, :], first + i, t)
-                    copy = on_vector if t % 2 == 0 else on_scalar
-                    copy(out=sb[:], in_=bank[:])
+                    if (first, t) == (GROUPS - 2, ROW_TILES - 1):
+                        for i, copy in enumerate((on_scalar, on_vector)):
+                            bank = banks.tile([P, COEFFS], F32, tag="bank", name="end_bank")
+                            second(bank[:], first + i, t)
+                            copy(out=sb[:, i, :], in_=bank[:])
+                    else:
+                        bank = banks.tile([P, 2, COEFFS], F32, tag="bank", name="out_bank")
+                        for i in range(2):
+                            second(bank[:, i, :], first + i, t)
+                        copy = on_vector if t % 2 == 0 else on_scalar
+                        copy(out=sb[:], in_=bank[:])
                     nc.sync.dma_start(
                         out=out_rows[:, t, first * COEFFS : (first + 2) * COEFFS], in_=sb[:].rearrange("p i r -> p (i r)")
                     )

@@ -21,7 +21,6 @@ WORDS = WINDOW // 2
 HALVES = WORDS // P
 PACK = 4
 HEAD_MATMULS = 3
-MID_PASSES = 2
 PAIR = 2
 
 FLOPS = 2 * SAMPLES * WINDOW * GROUPS * COEFFS + 2 * SAMPLES * GROUPS * COEFFS * COEFFS
@@ -51,13 +50,14 @@ def tile_switchnet_fstar_pb_s_kernel(tc, h_switch, k2, b2, k3, b3, grad_out, out
             k3_sb = keep.tile([P, GROUPS * WINDOW], BF16)
             k2_sb = keep.tile([P, GROUPS * COEFFS], BF16)
             dy_sb_tiles = dy_sb[:].rearrange("p (t l) -> p t l", t=ROW_TILES)
-            for h in range(ROW_TILES // PAIR):
-                tiles = slice(PAIR * h, PAIR * (h + 1))
+            for tiles in (slice(0, 1), slice(1, 2), slice(2, 4)):
                 nc.sync.dma_start(out=dy_sb_tiles[:, tiles, :], in_=dy_rows[:, tiles, :])
             for j in range(GROUPS):
                 nc.sync.dma_start(out=k3_sb[:, j * WINDOW : (j + 1) * WINDOW], in_=k3_rows[:, j, :])
             nc.sync.dma_start(out=k2_sb[:], in_=k2_rows)
 
+            ones = keep.tile([P, P], F32)
+            nc.vector.memset(ones[:], 1.0)
             identity_f32 = keep.tile([P, P], F32)
             make_identity(nc, identity_f32[:])
             identity_bf16 = keep.tile([P, P], BF16)
@@ -65,7 +65,7 @@ def tile_switchnet_fstar_pb_s_kernel(tc, h_switch, k2, b2, k3, b3, grad_out, out
 
             idle_bank = banks.tile([P, SAMPLES], F32, tag="bank")
             for i in range(HEAD_MATMULS):
-                nc.tensor.matmul(out=idle_bank[:, 0:P], lhsT=identity_f32[:], rhs=identity_f32[:], start=True, stop=True)
+                nc.tensor.matmul(out=idle_bank[:, 0:P], lhsT=ones[:], rhs=ones[:], start=True, stop=True)
             zeros = keep.tile([P, SAMPLES * PACK], BF16, align_bytes=64)
             zero_moving = keep.tile([P, SAMPLES], U32, align_bytes=64)
             zero_moving_scales = keep.tile([P, SAMPLES], U8, align_bytes=64)
@@ -138,13 +138,7 @@ def tile_switchnet_fstar_pb_s_kernel(tc, h_switch, k2, b2, k3, b3, grad_out, out
                     stop=True,
                 )
 
-            transpose_and_group(dy_words, dy_grouped_words, 0, 2, on_scalar)
-            transpose_and_group(dy_words, dy_grouped_words, 2, 2, on_scalar)
-            quantise(dy_codes, dy_scales, dy_grouped, E5M2_X4, 0, 2)
-            quantise(dy_codes, dy_scales, dy_grouped, E5M2_X4, 2, 2)
-            transpose_and_group(k3_words, k3_grouped_words, 0, 1, on_scalar)
-            quantise(k3_codes, k3_scales, k3_grouped, E4M3_X4, 0, 1)
-            for i in range(MID_PASSES):
+            def idle_pass():
                 nc.tensor.matmul_mx(
                     out=idle_bank[:],
                     lhsT=zero_stationary[:].bitcast(E4M3_X4),
@@ -154,6 +148,17 @@ def tile_switchnet_fstar_pb_s_kernel(tc, h_switch, k2, b2, k3, b3, grad_out, out
                     start=True,
                     stop=True,
                 )
+
+            transpose_and_group(dy_words, dy_grouped_words, 0, 1, on_scalar)
+            transpose_and_group(dy_words, dy_grouped_words, 1, 1, on_scalar)
+            idle_pass()
+            transpose_and_group(dy_words, dy_grouped_words, 2, 1, on_vector)
+            quantise(dy_codes, dy_scales, dy_grouped, E5M2_X4, 0, 2)
+            transpose_and_group(dy_words, dy_grouped_words, 3, 1, on_scalar)
+            quantise(dy_codes, dy_scales, dy_grouped, E5M2_X4, 2, 2)
+            transpose_and_group(k3_words, k3_grouped_words, 0, 1, on_scalar)
+            quantise(k3_codes, k3_scales, k3_grouped, E4M3_X4, 0, 1)
+            idle_pass()
             for j in range(1, GROUPS):
                 transpose_and_group(k3_words, k3_grouped_words, j, 1, on_scalar)
                 quantise(k3_codes, k3_scales, k3_grouped, E4M3_X4, j, 1)
@@ -174,7 +179,7 @@ def tile_switchnet_fstar_pb_s_kernel(tc, h_switch, k2, b2, k3, b3, grad_out, out
                 for t in range(ROW_TILES):
                     sb = keep.tile([P, 2, COEFFS], F32, name="out_sb%d%d" % (first, t))
                     if (first, t) == (GROUPS - 2, ROW_TILES - 1):
-                        for i, copy in enumerate((on_scalar, on_vector)):
+                        for i, copy in enumerate((on_vector, on_scalar)):
                             bank = banks.tile([P, COEFFS], F32, tag="bank", name="end_bank")
                             second(bank[:], first + i, t)
                             copy(out=sb[:, i, :], in_=bank[:])

@@ -58,6 +58,20 @@ def tile_switchnet_fstar_pb_s_kernel(tc, h_switch, k2, b2, k3, b3, grad_out, out
 
             ones = keep.tile([P, P], F32)
             nc.vector.memset(ones[:], 1.0)
+            zeros = keep.tile([P, P * PACK], BF16, align_bytes=64)
+            zero_stationary = keep.tile([P, P], U32, align_bytes=64)
+            zero_stationary_scales = keep.tile([P, P], U8, align_bytes=64)
+            zero_moving = keep.tile([P, SAMPLES], U32, align_bytes=64)
+            zero_moving_scales = keep.tile([P, SAMPLES], U8, align_bytes=64)
+            nc.vector.memset(zeros[:].bitcast(I32), 0)
+            nc.vector.memset(zero_moving[:, P:].bitcast(I32), 0)
+            nc.vector.memset(zero_moving_scales[:, P:].bitcast(I32), 0)
+            nc.vector.quantize_mx(
+                out=zero_stationary[:].bitcast(E4M3_X4), scales=zero_stationary_scales[:], in_=zeros[:]
+            )
+            nc.vector.quantize_mx(
+                out=zero_moving[:, 0:P].bitcast(E5M2_X4), scales=zero_moving_scales[:, 0:P], in_=zeros[:]
+            )
             identity_f32 = keep.tile([P, P], F32)
             make_identity(nc, identity_f32[:])
             identity_bf16 = keep.tile([P, P], BF16)
@@ -66,17 +80,6 @@ def tile_switchnet_fstar_pb_s_kernel(tc, h_switch, k2, b2, k3, b3, grad_out, out
             idle_bank = banks.tile([P, SAMPLES], F32, tag="bank")
             for i in range(HEAD_MATMULS):
                 nc.tensor.matmul(out=idle_bank[:, 0:P], lhsT=ones[:], rhs=ones[:], start=True, stop=True)
-            zeros = keep.tile([P, SAMPLES * PACK], BF16, align_bytes=64)
-            zero_moving = keep.tile([P, SAMPLES], U32, align_bytes=64)
-            zero_moving_scales = keep.tile([P, SAMPLES], U8, align_bytes=64)
-            zero_stationary = keep.tile([P, P], U32, align_bytes=64)
-            zero_stationary_scales = keep.tile([P, P], U8, align_bytes=64)
-            nc.vector.memset(zeros[:].bitcast(I32), 0)
-            nc.vector.quantize_mx(out=zero_moving[:].bitcast(E5M2_X4), scales=zero_moving_scales[:], in_=zeros[:])
-            nc.vector.quantize_mx(
-                out=zero_stationary[:].bitcast(E4M3_X4), scales=zero_stationary_scales[:], in_=zeros[:, 0 : P * PACK]
-            )
-
             dy_words = dy_sb[:].bitcast(F32)
             dy_grouped = keep.tile([P, SAMPLES * PACK], BF16, align_bytes=64)
             dy_grouped_words = dy_grouped[:].bitcast(F32)

from contextlib import ExitStack

import concourse.mybir as mybir
from concourse.masks import make_identity

F32 = mybir.dt.float32
BF16 = mybir.dt.bfloat16
U32 = mybir.dt.uint32
U8 = mybir.dt.uint8
I32 = mybir.dt.int32
E4M3_X4 = mybir.dt.float8_e4m3fn_x4
E5M2_X4 = mybir.dt.float8_e5m2_x4

P = 128
SAMPLES = 512
WINDOW = 512
GROUPS = 4
COEFFS = 128
ROW_TILES = SAMPLES // P
WORDS = WINDOW // 2
HALVES = WORDS // P
PACK = 4
HEAD_MATMULS = 3
PAIR = 2

FLOPS = 2 * SAMPLES * WINDOW * GROUPS * COEFFS + 2 * SAMPLES * GROUPS * COEFFS * COEFFS
BYTES = 2 * (SAMPLES * WINDOW + GROUPS * COEFFS * WINDOW + GROUPS * COEFFS * COEFFS) + 4 * SAMPLES * GROUPS * COEFFS


def transpose_row_tile(nc, bank, words, identity):
    for u in range(HALVES):
        nc.tensor.transpose(out=bank[:, u, :], in_=words[:, u * P : (u + 1) * P], identity=identity)


def tile_switchnet_fstar_pb_s_kernel(tc, h_switch, k2, b2, k3, b3, grad_out, out):
    nc = tc.nc
    on_vector = nc.vector.tensor_copy
    on_scalar = nc.scalar.copy
    with ExitStack() as ctx:
        keep = ctx.enter_context(tc.tile_pool(name="keep", bufs=1))
        banks = ctx.enter_context(tc.psum_pool(name="banks", bufs=8))

        with tc.manual_schedule():
            dy_rows = grad_out.rearrange("(p t) x y c -> p t (x y c)", t=ROW_TILES)
            k3_rows = k3.rearrange("o (j p) l -> p (o j) l", p=P)
            k2_rows = k2.rearrange("j (q t) r -> (j q) (t r)", t=GROUPS)
            out_rows = out.rearrange("(p t) j r -> p t (j r)", t=ROW_TILES)

            dy_sb = keep.tile([P, ROW_TILES * WINDOW], BF16)
            k3_sb = keep.tile([P, GROUPS * WINDOW], BF16)
            k2_sb = keep.tile([P, GROUPS * COEFFS], BF16)
            dy_sb_tiles = dy_sb[:].rearrange("p (t l) -> p t l", t=ROW_TILES)
            for tiles in (slice(0, 1), slice(1, 2), slice(2, 4)):
                nc.sync.dma_start(out=dy_sb_tiles[:, tiles, :], in_=dy_rows[:, tiles, :])
            for j in range(GROUPS):
                nc.sync.dma_start(out=k3_sb[:, j * WINDOW : (j + 1) * WINDOW], in_=k3_rows[:, j, :])
            nc.sync.dma_start(out=k2_sb[:], in_=k2_rows)

            ones = keep.tile([P, P], F32)
            nc.vector.memset(ones[:], 1.0)
            zeros = keep.tile([P, P * PACK], BF16, align_bytes=64)
            zero_stationary = keep.tile([P, P], U32, align_bytes=64)
            zero_stationary_scales = keep.tile([P, P], U8, align_bytes=64)
            zero_moving = keep.tile([P, SAMPLES], U32, align_bytes=64)
            zero_moving_scales = keep.tile([P, SAMPLES], U8, align_bytes=64)
            nc.vector.memset(zeros[:].bitcast(I32), 0)
            nc.vector.memset(zero_moving[:, P:].bitcast(I32), 0)
            nc.vector.memset(zero_moving_scales[:, P:].bitcast(I32), 0)
            nc.vector.quantize_mx(
                out=zero_stationary[:].bitcast(E4M3_X4), scales=zero_stationary_scales[:], in_=zeros[:]
            )
            nc.vector.quantize_mx(
                out=zero_moving[:, 0:P].bitcast(E5M2_X4), scales=zero_moving_scales[:, 0:P], in_=zeros[:]
            )
            identity_f32 = keep.tile([P, P], F32)
            make_identity(nc, identity_f32[:])
            identity_bf16 = keep.tile([P, P], BF16)
            nc.vector.tensor_copy(out=identity_bf16[:], in_=identity_f32[:])

            idle_bank = banks.tile([P, SAMPLES], F32, tag="bank")
            for i in range(HEAD_MATMULS):
                nc.tensor.matmul(out=idle_bank[:, 0:P], lhsT=ones[:], rhs=ones[:], start=True, stop=True)
            dy_words = dy_sb[:].bitcast(F32)
            dy_grouped = keep.tile([P, SAMPLES * PACK], BF16, align_bytes=64)
            dy_grouped_words = dy_grouped[:].bitcast(F32)
            dy_codes = keep.tile([P, SAMPLES], U32, align_bytes=64)
            dy_scales = keep.tile([P, SAMPLES], U8, align_bytes=64)
            k3_words = k3_sb[:].bitcast(F32)
            k3_grouped = keep.tile([P, GROUPS * COEFFS * PACK], BF16, align_bytes=64)
            k3_grouped_words = k3_grouped[:].bitcast(F32)
            k3_codes = keep.tile([P, GROUPS * COEFFS], U32, align_bytes=64)
            k3_scales = keep.tile([P, GROUPS * COEFFS], U8, align_bytes=64)
            k2T = keep.tile([P, GROUPS * COEFFS], F32)
            dgT = [keep.tile([P, SAMPLES], F32, name="dgT%d" % j) for j in range(GROUPS)]

            def transpose_and_group(words, grouped_words, first, count, engine_copy):
                bank = banks.tile([P, count, HALVES, P], F32, tag="bank", name="t_bank")
                for i in range(count):
                    transpose_row_tile(
                        nc, bank[:, i], words[:, (first + i) * WORDS : (first + i + 1) * WORDS], identity_f32[:]
                    )
                engine_copy(
                    out=grouped_words[:, first * WORDS : (first + count) * WORDS].rearrange(
                        "p (t r u) -> p t r u", t=count, u=HALVES
                    ),
                    in_=bank[:].rearrange("p t u r -> p t r u"),
                )

            def quantise(codes, scales, grouped, fmt, first, count):
                cols = slice(first * P, (first + count) * P)
                nc.vector.quantize_mx(
                    out=codes[:, cols].bitcast(fmt),
                    scales=scales[:, cols],
                    in_=grouped[:, first * P * PACK : (first + count) * P * PACK],
                )

            def mx_pass(j):
                cols = slice(j * COEFFS, (j + 1) * COEFFS)
                bank = banks.tile([P, SAMPLES], F32, tag="bank", name="dg_bank")
                nc.tensor.matmul_mx(
                    out=bank[:],
                    lhsT=k3_codes[:, cols].bitcast(E4M3_X4),
                    lhsT_scale=k3_scales[:, cols],
                    rhs=dy_codes[:].bitcast(E5M2_X4),
                    rhs_scale=dy_scales[:],
                    start=True,
                    stop=True,
                )
                return bank

            def leave(j, bank, first, count, engine_copy):
                cols = slice(first * P, (first + count) * P)
                engine_copy(out=dgT[j][:, cols], in_=bank[:, cols])

            def second(dst, j, t):
                nc.tensor.matmul(
                    out=dst,
                    lhsT=dgT[j][:, t * P : (t + 1) * P],
                    rhs=k2T[:, j * COEFFS : (j + 1) * COEFFS],
                    start=True,
                    stop=True,
                )

            def idle_pass():
                nc.tensor.matmul_mx(
                    out=idle_bank[:],
                    lhsT=zero_stationary[:].bitcast(E4M3_X4),
                    lhsT_scale=zero_stationary_scales[:],
                    rhs=zero_moving[:].bitcast(E5M2_X4),
                    rhs_scale=zero_moving_scales[:],
                    start=True,
                    stop=True,
                )

            transpose_and_group(dy_words, dy_grouped_words, 0, 1, on_scalar)
            transpose_and_group(dy_words, dy_grouped_words, 1, 1, on_scalar)
            idle_pass()
            transpose_and_group(dy_words, dy_grouped_words, 2, 1, on_vector)
            quantise(dy_codes, dy_scales, dy_grouped, E5M2_X4, 0, 2)
            transpose_and_group(dy_words, dy_grouped_words, 3, 1, on_scalar)
            quantise(dy_codes, dy_scales, dy_grouped, E5M2_X4, 2, 2)
            transpose_and_group(k3_words, k3_grouped_words, 0, 1, on_scalar)
            quantise(k3_codes, k3_scales, k3_grouped, E4M3_X4, 0, 1)
            idle_pass()
            for j in range(1, GROUPS):
                transpose_and_group(k3_words, k3_grouped_words, j, 1, on_scalar)
                quantise(k3_codes, k3_scales, k3_grouped, E4M3_X4, j, 1)
            k2_bank = banks.tile([P, GROUPS, P], BF16, tag="bank")
            for t in range(GROUPS):
                nc.tensor.transpose(
                    out=k2_bank[:, t, :], in_=k2_sb[:, t * COEFFS : (t + 1) * COEFFS], identity=identity_bf16[:]
                )
            nc.scalar.copy(out=k2T[:].rearrange("r (p t) -> r p t", t=GROUPS), in_=k2_bank[:].rearrange("r t p -> r p t"))

            dg = [mx_pass(j) for j in range(GROUPS)]
            for first in range(0, GROUPS, 2):
                for half in range(2):
                    leave(first, dg[first], 2 * half, 2, on_vector)
                    leave(first + 1, dg[first + 1], 2 * half, 2, on_scalar)

            for first in range(0, GROUPS, 2):
                for t in range(ROW_TILES):
                    sb = keep.tile([P, 2, COEFFS], F32, name="out_sb%d%d" % (first, t))
                    if (first, t) == (GROUPS - 2, ROW_TILES - 1):
                        for i, copy in enumerate((on_vector, on_scalar)):
                            bank = banks.tile([P, COEFFS], F32, tag="bank", name="end_bank")
                            second(bank[:], first + i, t)
                            copy(out=sb[:, i, :], in_=bank[:])
                    else:
                        bank = banks.tile([P, 2, COEFFS], F32, tag="bank", name="out_bank")
                        for i in range(2):
                            second(bank[:, i, :], first + i, t)
                        copy = on_vector if t % 2 == 0 else on_scalar
                        copy(out=sb[:], in_=bank[:])
                    nc.sync.dma_start(
                        out=out_rows[:, t, first * COEFFS : (first + 2) * COEFFS], in_=sb[:].rearrange("p i r -> p (i r)")
                    )
